import numpy as np
import ml_dtypes


def mxq(x, axis, fmt="e4m3"):
    dtype, down = {"e4m3": (ml_dtypes.float8_e4m3fn, 7), "e5m2": (ml_dtypes.float8_e5m2, 14)}[fmt]
    v = np.moveaxis(np.asarray(x, np.float32).astype(ml_dtypes.bfloat16).astype(np.float64), axis, -1)
    blocks = v.reshape(v.shape[:-1] + (-1, 32))
    amax = np.abs(blocks).max(-1, keepdims=True)
    byte = np.maximum(np.where(amax > 0, np.frexp(amax)[1] - 1 + 127, 0) - down, 1)
    scale = np.exp2(byte - 127.0)
    codes = (blocks / scale).astype(np.float32).astype(dtype).astype(np.float64)
    return np.moveaxis((codes * scale).reshape(v.shape), -1, axis)


WIDE = False


def mx_kscale(k):
    if not WIDE:
        return np.ones(k)
    levels = np.array([10, -10, 5, -5, 0])
    a = np.random.permutation(np.resize(levels, k // 512 * 4)).reshape(k // 512, 4)
    idx = np.arange(k)
    return np.exp2(a[idx // 512, idx % 128 // 32])


BF16 = ml_dtypes.bfloat16


def bf(x):
    return np.asarray(x, np.float32).astype(BF16)


def f64(x):
    return np.asarray(x).astype(np.float64)


E2M1 = np.array([0.0, 0.5, 1.0, 1.5, 2.0, 3.0, 4.0, 6.0, -0.0, -0.5, -1.0, -1.5, -2.0, -3.0, -4.0, -6.0])


def pack_weight(w, fmt):
    k, n = w.shape
    w = f64(bf(w)).reshape(k // 32, 32, n)
    amax = np.abs(w).max(1)
    if fmt == "e4m3":
        byte = np.frexp(amax)[1] - 1 + 127 - 7
    else:
        mant, ex = np.frexp(amax / 6.0)
        byte = np.where(mant > 0.5, ex, ex - 1) + 127
    byte = np.clip(np.where(amax > 0, byte, 1), 1, 254)
    scaled = (w * np.exp2(127.0 - byte)[:, None, :]).reshape(k, n).astype(np.float32)
    by_word = np.ascontiguousarray(scaled.reshape(k // 512, 128, 4, n).transpose(0, 1, 3, 2))
    if fmt == "e4m3":
        words = by_word.astype(ml_dtypes.float8_e4m3fn).view(np.uint8)
    else:
        c = by_word.astype(ml_dtypes.float4_e2m1fn).view(np.uint8) & 0xF
        words = c[..., 0::2] | (c[..., 1::2] << 4)
    return np.ascontiguousarray(words), np.ascontiguousarray(byte.astype(np.uint8).reshape(k // 512, 16, n))


def unpack_weight(words, scales, fmt):
    g, p, n, _ = words.shape
    if fmt == "e4m3":
        vals = np.ascontiguousarray(words).view(ml_dtypes.float8_e4m3fn).astype(np.float64)
    else:
        nib = np.empty((g, p, n, 4), np.uint8)
        nib[..., 0::2] = words & 0xF
        nib[..., 1::2] = words >> 4
        vals = E2M1[nib]
    vals = vals * np.repeat(np.exp2(scales.astype(np.float64) - 127.0), 8, axis=1)[..., None]
    return vals.transpose(0, 1, 3, 2).reshape(g * 512, n)


N, H, W, K = 128, 256, 4, 16384
TAU = 1.0


def silu(v):
    return v / (1.0 + np.exp(-v))


def softmax_last(v):
    e = np.exp(v - v.max(-1, keepdims=True))
    return e / e.sum(-1, keepdims=True)


def setup_inputs():
    s = np.tile(mx_kscale(K), W)
    x = bf(np.random.standard_normal((N, W * K)) * s)
    t = np.random.standard_normal((H, W * K)) / np.sqrt(K) / s
    words, scales = pack_weight(np.ascontiguousarray(t.T), "e4m3")
    return {"x": x, "template_flat_words": words, "template_flat_scales": scales}


def reference(x, template_flat_words, template_flat_scales):
    n = x.shape[0]
    xw = f64(x).reshape(n, W, K)
    xq = mxq(xw, 2, "e4m3")
    tq = unpack_weight(template_flat_words, template_flat_scales, "e4m3").reshape(W, K, -1)
    s = (xq.transpose(1, 0, 2) @ tq).transpose(1, 2, 0)
    gate = softmax_last(s / TAU)
    return np.sum(gate * silu(s), axis=-1)

@@ -1,0 +1,181 @@
+from contextlib import ExitStack
+
+import concourse.mybir as mybir
+from concourse.masks import make_identity
+
+F32 = mybir.dt.float32
+BF16 = mybir.dt.bfloat16
+I32 = mybir.dt.int32
+U32 = mybir.dt.uint32
+U8 = mybir.dt.uint8
+FP8X4 = mybir.dt.float8_e4m3fn_x4
+ACT = mybir.ActivationFunctionType
+ALU = mybir.AluOpType
+
+P = 128
+ROWS = 128
+FEATURES = 256
+WINDOWS = 4
+WINDOW_K = 16384
+PACK = 4
+K_PASS = P * PACK
+PASSES = WINDOW_K // K_PASS
+PAIR = 2
+PASS_WORDS = K_PASS // PAIR
+
+ROUND = 4
+ROUNDS = PASSES // ROUND
+BANK_PASSES = 2
+BANKS = ROUND // BANK_PASSES
+CHUNK = 16
+CHUNK_ROUNDS = CHUNK // ROUND
+CHUNKS = PASSES // CHUNK
+QUADRANT = 32
+PLANE_ROWS = 4
+
+FLOPS = 2 * ROWS * FEATURES * WINDOWS * WINDOW_K
+
+
+def load_weight_scales(nc, keep, scales, w):
+    w_planes = keep.tile([P, PASSES * FEATURES], U8, name="w_planes%d" % w, align_bytes=64)
+    nc.vector.memset(w_planes[:].bitcast(I32), 0)
+    by_row = scales[w * PASSES : (w + 1) * PASSES].rearrange("g (q r) h -> r q g h", r=PLANE_ROWS)
+    for r in range(PLANE_ROWS):
+        nc.gpsimd.dma_start(
+            out=w_planes[PLANE_ROWS * w + r : P : QUADRANT, :].bitcast(F32).rearrange("q (g h) -> q g h", g=PASSES),
+            in_=by_row[r].bitcast(F32),
+        )
+    return w_planes
+
+
+def load_x_window(nc, x_pool, x, w):
+    x_chunks = []
+    for c in range(CHUNKS):
+        first_k = w * WINDOW_K + c * CHUNK * K_PASS
+        x_chunk = x_pool.tile([P, CHUNK * K_PASS], BF16)
+        nc.sync.dma_start(out=x_chunk[:], in_=x[:, first_k : first_k + CHUNK * K_PASS])
+        x_chunks.append(x_chunk)
+    return x_chunks
+
+
+def load_weight_window(nc, w_pool, words, w):
+    w_rounds = []
+    for r in range(ROUNDS):
+        first_pass = w * PASSES + r * ROUND
+        w_round = w_pool.tile([P, ROUND, FEATURES], U32, align_bytes=64)
+        nc.sync.dma_start(
+            out=w_round[:].bitcast(I32),
+            in_=words[first_pass : first_pass + ROUND].rearrange("g p h t -> p g (h t)").bitcast(I32),
+        )
+        w_rounds.append(w_round)
+    return w_rounds
+
+
+def quantise_x_window(nc, code_pool, grouped_pool, bank_pool, ident, x_chunks):
+    x_codes = code_pool.tile([P, PASSES * ROWS], U32, align_bytes=64)
+    x_planes = code_pool.tile([P, PASSES * ROWS], U8, align_bytes=64)
+
+    def quantise_round(r, grouped):
+        cols = slice(r * ROUND * ROWS, (r + 1) * ROUND * ROWS)
+        nc.vector.quantize_mx(out=x_codes[:, cols].bitcast(FP8X4), scales=x_planes[:, cols], in_=grouped[:])
+
+    earlier = None
+    for r in range(ROUNDS):
+        x_words = x_chunks[r // CHUNK_ROUNDS][:].bitcast(F32)
+        grouped = grouped_pool.tile([P, ROUND * ROWS * PACK], BF16, align_bytes=64)
+        grouped_words = grouped[:].bitcast(F32).rearrange("p (a n u) -> p a n u", n=ROWS, u=PAIR)
+        for b in range(BANKS):
+            bank = bank_pool.tile([P, BANK_PASSES, PAIR, ROWS], F32)
+            for a in range(BANK_PASSES):
+                first_word = ((r % CHUNK_ROUNDS) * ROUND + b * BANK_PASSES + a) * PASS_WORDS
+                for u in range(PAIR):
+                    nc.tensor.transpose(
+                        out=bank[:, a, u, :],
+                        in_=x_words[:, first_word + u : first_word + PASS_WORDS : PAIR],
+                        identity=ident[:],
+                    )
+            passes = slice(b * BANK_PASSES, (b + 1) * BANK_PASSES)
+            if b % 2 == 0:
+                nc.scalar.copy(out=grouped_words[:, passes], in_=bank[:].rearrange("p a u n -> p a n u"))
+            else:
+                nc.vector.tensor_copy(out=grouped_words[:, passes], in_=bank[:].rearrange("p a u n -> p a n u"))
+        if r > 0:
+            quantise_round(r - 1, earlier)
+        earlier = grouped
+    quantise_round(ROUNDS - 1, earlier)
+    return x_codes, x_planes
+
+
+def score_window(nc, score, x_codes, x_planes, w_rounds, w_planes, w):
+    for g in range(PASSES):
+        rows = slice(g * ROWS, (g + 1) * ROWS)
+        nc.tensor.matmul_mx(
+            out=score[:],
+            lhsT=x_codes[:, rows].bitcast(FP8X4),
+            lhsT_scale=x_planes[:, rows],
+            rhs=w_rounds[g // ROUND][:, g % ROUND, :].bitcast(FP8X4),
+            rhs_scale=w_planes[PLANE_ROWS * w : P, g * FEATURES : (g + 1) * FEATURES],
+            start=(g == 0),
+            stop=(g == PASSES - 1),
+        )
+
+
+def fold_window(nc, work, lse, avg, score, w):
+    sig = work.tile([P, FEATURES], F32)
+    if w == 0:
+        nc.scalar.activation(out=sig[:], in_=score[:], func=ACT.Sigmoid)
+        nc.vector.tensor_copy(out=lse[:], in_=score[:])
+        nc.vector.tensor_mul(out=avg[:], in0=lse[:], in1=sig[:])
+        return
+    share = work.tile([P, FEATURES], F32)
+    nc.vector.tensor_sub(out=share[:], in0=score[:], in1=lse[:])
+    nc.scalar.activation(out=share[:], in_=share[:], func=ACT.Sigmoid)
+    if w < WINDOWS - 1:
+        larger = work.tile([P, FEATURES], F32)
+        nc.vector.tensor_max(out=lse[:], in0=score[:], in1=lse[:])
+        nc.vector.tensor_scalar(out=larger[:], in0=share[:], scalar1=-1.0, scalar2=1.0, op0=ALU.mult, op1=ALU.add)
+        nc.vector.tensor_max(out=larger[:], in0=larger[:], in1=share[:])
+        nc.scalar.activation(out=larger[:], in_=larger[:], func=ACT.Ln)
+        nc.vector.tensor_sub(out=lse[:], in0=lse[:], in1=larger[:])
+    step = work.tile([P, FEATURES], F32)
+    nc.scalar.activation(out=sig[:], in_=score[:], func=ACT.Sigmoid)
+    nc.vector.tensor_mul(out=step[:], in0=score[:], in1=sig[:])
+    nc.vector.tensor_sub(out=step[:], in0=step[:], in1=avg[:])
+    nc.vector.tensor_mul(out=step[:], in0=step[:], in1=share[:])
+    nc.vector.tensor_add(out=avg[:], in0=avg[:], in1=step[:])
+
+
+def tile_dendriticlayersilu_ffn_k_kernel(tc, x, template_flat_words, template_flat_scales, out):
+    nc = tc.nc
+    with ExitStack() as ctx:
+        keep = ctx.enter_context(tc.tile_pool(name="keep", bufs=1))
+        x_pool = ctx.enter_context(tc.tile_pool(name="x", bufs=2 * CHUNKS))
+        w_pool = ctx.enter_context(tc.tile_pool(name="w", bufs=2 * ROUNDS))
+        code_pool = ctx.enter_context(tc.tile_pool(name="codes", bufs=2))
+        grouped_pool = ctx.enter_context(tc.tile_pool(name="grouped", bufs=3))
+        work = ctx.enter_context(tc.tile_pool(name="work", bufs=2))
+        score_pool = ctx.enter_context(tc.psum_pool(name="score", bufs=1))
+        bank_pool = ctx.enter_context(tc.psum_pool(name="bank", bufs=4))
+        ctx.enter_context(tc.manual_schedule())
+
+        ident = keep.tile([P, P], F32)
+        make_identity(nc, ident[:])
+        w_planes = [load_weight_scales(nc, keep, template_flat_scales, w) for w in range(WINDOWS)]
+
+        lse = keep.tile([P, FEATURES], F32)
+        avg = keep.tile([P, FEATURES], F32)
+
+        x_chunks = load_x_window(nc, x_pool, x, 0)
+        ahead = quantise_x_window(nc, code_pool, grouped_pool, bank_pool, ident, x_chunks)
+        for w in range(WINDOWS):
+            x_codes, x_planes = ahead
+            if w + 1 < WINDOWS:
+                x_chunks = load_x_window(nc, x_pool, x, w + 1)
+            w_rounds = load_weight_window(nc, w_pool, template_flat_words, w)
+            if w + 1 < WINDOWS:
+                ahead = quantise_x_window(nc, code_pool, grouped_pool, bank_pool, ident, x_chunks)
+            score = score_pool.tile([P, FEATURES], F32, name="score%d" % w)
+            score_window(nc, score, x_codes, x_planes, w_rounds, w_planes[w], w)
+            fold_window(nc, work, lse, avg, score, w)
+
+        nc.sync.dma_start(out=out[:, :], in_=avg[:])

@@ -27,6 +27,7 @@ ROUND = 4
 ROUNDS = PASSES // ROUND
 BANK_PASSES = 2
 BANKS = ROUND // BANK_PASSES
+VECTOR_EVERY = 4
 CHUNK = 16
 CHUNK_ROUNDS = CHUNK // ROUND
 CHUNKS = PASSES // CHUNK
@@ -95,10 +96,10 @@ def quantise_x_window(nc, code_pool, grouped_pool, bank_pool, ident, x_chunks):
                         identity=ident[:],
                     )
             passes = slice(b * BANK_PASSES, (b + 1) * BANK_PASSES)
-            if b % 2 == 0:
-                nc.scalar.copy(out=grouped_words[:, passes], in_=bank[:].rearrange("p a u n -> p a n u"))
-            else:
+            if (r * BANKS + b) % VECTOR_EVERY == VECTOR_EVERY - 1:
                 nc.vector.tensor_copy(out=grouped_words[:, passes], in_=bank[:].rearrange("p a u n -> p a n u"))
+            else:
+                nc.scalar.copy(out=grouped_words[:, passes], in_=bank[:].rearrange("p a u n -> p a n u"))
         if r > 0:
             quantise_round(r - 1, earlier)
         earlier = grouped
@@ -154,8 +155,8 @@ def tile_dendriticlayersilu_ffn_k_kernel(tc, x, template_flat_words, template_fl
         code_pool = ctx.enter_context(tc.tile_pool(name="codes", bufs=2))
         grouped_pool = ctx.enter_context(tc.tile_pool(name="grouped", bufs=3))
         work = ctx.enter_context(tc.tile_pool(name="work", bufs=2))
-        score_pool = ctx.enter_context(tc.psum_pool(name="score", bufs=1))
-        bank_pool = ctx.enter_context(tc.psum_pool(name="bank", bufs=4))
+        score_pool = ctx.enter_context(tc.psum_pool(name="score", bufs=2))
+        bank_pool = ctx.enter_context(tc.psum_pool(name="bank", bufs=6))
         ctx.enter_context(tc.manual_schedule())
 
         ident = keep.tile([P, P], F32)
@@ -174,7 +175,7 @@ def tile_dendriticlayersilu_ffn_k_kernel(tc, x, template_flat_words, template_fl
             w_rounds = load_weight_window(nc, w_pool, template_flat_words, w)
             if w + 1 < WINDOWS:
                 ahead = quantise_x_window(nc, code_pool, grouped_pool, bank_pool, ident, x_chunks)
-            score = score_pool.tile([P, FEATURES], F32, name="score%d" % w)
+            score = score_pool.tile([P, FEATURES], F32)
             score_window(nc, score, x_codes, x_planes, w_rounds, w_planes[w], w)
             fold_window(nc, work, lse, avg, score, w)
 

@@ -123,14 +123,19 @@ def score_window(nc, score, x_codes, x_planes, w_rounds, w_planes, w):
 
 def fold_window(nc, work, lse, avg, score, w):
     sig = work.tile([P, FEATURES], F32)
+    nc.scalar.activation(out=sig[:], in_=score[:], func=ACT.Sigmoid)
     if w == 0:
-        nc.scalar.activation(out=sig[:], in_=score[:], func=ACT.Sigmoid)
         nc.vector.tensor_copy(out=lse[:], in_=score[:])
         nc.vector.tensor_mul(out=avg[:], in0=lse[:], in1=sig[:])
         return
     share = work.tile([P, FEATURES], F32)
+    step = work.tile([P, FEATURES], F32)
     nc.vector.tensor_sub(out=share[:], in0=score[:], in1=lse[:])
     nc.scalar.activation(out=share[:], in_=share[:], func=ACT.Sigmoid)
+    nc.vector.tensor_mul(out=step[:], in0=score[:], in1=sig[:])
+    nc.vector.tensor_sub(out=step[:], in0=step[:], in1=avg[:])
+    nc.vector.tensor_mul(out=step[:], in0=step[:], in1=share[:])
+    nc.vector.tensor_add(out=avg[:], in0=avg[:], in1=step[:])
     if w < WINDOWS - 1:
         larger = work.tile([P, FEATURES], F32)
         nc.vector.tensor_max(out=lse[:], in0=score[:], in1=lse[:])
@@ -138,12 +143,6 @@ def fold_window(nc, work, lse, avg, score, w):
         nc.vector.tensor_max(out=larger[:], in0=larger[:], in1=share[:])
         nc.scalar.activation(out=larger[:], in_=larger[:], func=ACT.Ln)
         nc.vector.tensor_sub(out=lse[:], in0=lse[:], in1=larger[:])
-    step = work.tile([P, FEATURES], F32)
-    nc.scalar.activation(out=sig[:], in_=score[:], func=ACT.Sigmoid)
-    nc.vector.tensor_mul(out=step[:], in0=score[:], in1=sig[:])
-    nc.vector.tensor_sub(out=step[:], in0=step[:], in1=avg[:])
-    nc.vector.tensor_mul(out=step[:], in0=step[:], in1=share[:])
-    nc.vector.tensor_add(out=avg[:], in0=avg[:], in1=step[:])
 
 
 def tile_dendriticlayersilu_ffn_k_kernel(tc, x, template_flat_words, template_flat_scales, out):

@@ -37,16 +37,19 @@ PLANE_ROWS = 4
 FLOPS = 2 * ROWS * FEATURES * WINDOWS * WINDOW_K
 
 
-def load_weight_scales(nc, keep, scales, w):
+def zeroed_planes(nc, keep, w):
     w_planes = keep.tile([P, PASSES * FEATURES], U8, name="w_planes%d" % w, align_bytes=64)
     nc.vector.memset(w_planes[:].bitcast(I32), 0)
+    return w_planes
+
+
+def load_weight_scales(nc, w_planes, scales, w):
     by_row = scales[w * PASSES : (w + 1) * PASSES].rearrange("g (q r) h -> r q g h", r=PLANE_ROWS)
     for r in range(PLANE_ROWS):
-        nc.gpsimd.dma_start(
-            out=w_planes[PLANE_ROWS * w + r : P : QUADRANT, :].bitcast(F32).rearrange("q (g h) -> q g h", g=PASSES),
-            in_=by_row[r].bitcast(F32),
+        nc.sync.dma_start(
+            out=w_planes[PLANE_ROWS * w + r : P : QUADRANT, :].bitcast(I32).rearrange("q (g h) -> q g h", g=PASSES),
+            in_=by_row[r].bitcast(I32),
         )
-    return w_planes
 
 
 def load_x_window(nc, x_pool, x, w):
@@ -160,7 +163,7 @@ def tile_dendriticlayersilu_ffn_k_kernel(tc, x, template_flat_words, template_fl
 
         ident = keep.tile([P, P], F32)
         make_identity(nc, ident[:])
-        w_planes = [load_weight_scales(nc, keep, template_flat_scales, w) for w in range(WINDOWS)]
+        w_planes = [zeroed_planes(nc, keep, w) for w in range(WINDOWS)]
 
         lse = keep.tile([P, FEATURES], F32)
         avg = keep.tile([P, FEATURES], F32)
@@ -171,6 +174,7 @@ def tile_dendriticlayersilu_ffn_k_kernel(tc, x, template_flat_words, template_fl
             x_codes, x_planes = ahead
             if w + 1 < WINDOWS:
                 x_chunks = load_x_window(nc, x_pool, x, w + 1)
+            load_weight_scales(nc, w_planes[w], template_flat_scales, w)
             w_rounds = load_weight_window(nc, w_pool, template_flat_words, w)
             if w + 1 < WINDOWS:
                 ahead = quantise_x_window(nc, code_pool, grouped_pool, bank_pool, ident, x_chunks)

@@ -33,32 +33,34 @@ CHUNK_ROUNDS = CHUNK // ROUND
 CHUNKS = PASSES // CHUNK
 QUADRANT = 32
 PLANE_ROWS = 4
+SCALE_ROWS = K_PASS // 32
+LEAD_LOADS = 2 * CHUNKS
+LEAD_ROWS = SCALE_ROWS // LEAD_LOADS
 
 FLOPS = 2 * ROWS * FEATURES * WINDOWS * WINDOW_K
 
 
-def zeroed_planes(nc, keep, w):
-    w_planes = keep.tile([P, PASSES * FEATURES], U8, name="w_planes%d" % w, align_bytes=64)
-    nc.vector.memset(w_planes[:].bitcast(I32), 0)
-    return w_planes
+def load_scale_row(nc, w_planes, scales, q):
+    first = QUADRANT * (q // PLANE_ROWS) + q % PLANE_ROWS
+    nc.sync.dma_start(
+        out=w_planes[first : first + PLANE_ROWS * WINDOWS : PLANE_ROWS, :]
+        .bitcast(I32)
+        .rearrange("w (g h) -> w g h", g=PASSES),
+        in_=scales.rearrange("(w g) q h -> q w g h", w=WINDOWS)[q].bitcast(I32),
+    )
 
 
-def load_weight_scales(nc, w_planes, scales, w):
-    by_row = scales[w * PASSES : (w + 1) * PASSES].rearrange("g (q r) h -> r q g h", r=PLANE_ROWS)
-    for r in range(PLANE_ROWS):
-        nc.sync.dma_start(
-            out=w_planes[PLANE_ROWS * w + r : P : QUADRANT, :].bitcast(I32).rearrange("q (g h) -> q g h", g=PASSES),
-            in_=by_row[r].bitcast(I32),
-        )
-
-
-def load_x_window(nc, x_pool, x, w):
+def load_x_window(nc, x_pool, x, w, w_planes, scales):
     x_chunks = []
     for c in range(CHUNKS):
         first_k = w * WINDOW_K + c * CHUNK * K_PASS
         x_chunk = x_pool.tile([P, CHUNK * K_PASS], BF16)
         nc.sync.dma_start(out=x_chunk[:], in_=x[:, first_k : first_k + CHUNK * K_PASS])
         x_chunks.append(x_chunk)
+        lead = w * CHUNKS + c
+        if lead < LEAD_LOADS:
+            for q in range(lead * LEAD_ROWS, (lead + 1) * LEAD_ROWS):
+                load_scale_row(nc, w_planes, scales, q)
     return x_chunks
 
 
@@ -163,23 +165,23 @@ def tile_dendriticlayersilu_ffn_k_kernel(tc, x, template_flat_words, template_fl
 
         ident = keep.tile([P, P], F32)
         make_identity(nc, ident[:])
-        w_planes = [zeroed_planes(nc, keep, w) for w in range(WINDOWS)]
+        w_planes = keep.tile([P, PASSES * FEATURES], U8, align_bytes=64)
+        nc.vector.memset(w_planes[:].bitcast(I32), 0)
 
         lse = keep.tile([P, FEATURES], F32)
         avg = keep.tile([P, FEATURES], F32)
 
-        x_chunks = load_x_window(nc, x_pool, x, 0)
+        x_chunks = load_x_window(nc, x_pool, x, 0, w_planes, template_flat_scales)
         ahead = quantise_x_window(nc, code_pool, grouped_pool, bank_pool, ident, x_chunks)
         for w in range(WINDOWS):
             x_codes, x_planes = ahead
             if w + 1 < WINDOWS:
-                x_chunks = load_x_window(nc, x_pool, x, w + 1)
-            load_weight_scales(nc, w_planes[w], template_flat_scales, w)
+                x_chunks = load_x_window(nc, x_pool, x, w + 1, w_planes, template_flat_scales)
             w_rounds = load_weight_window(nc, w_pool, template_flat_words, w)
             if w + 1 < WINDOWS:
                 ahead = quantise_x_window(nc, code_pool, grouped_pool, bank_pool, ident, x_chunks)
             score = score_pool.tile([P, FEATURES], F32)
-            score_window(nc, score, x_codes, x_planes, w_rounds, w_planes[w], w)
+            score_window(nc, score, x_codes, x_planes, w_rounds, w_planes, w)
             fold_window(nc, work, lse, avg, score, w)
 
         nc.sync.dma_start(out=out[:, :], in_=avg[:])

@@ -35,19 +35,25 @@ QUADRANT = 32
 PLANE_ROWS = 4
 SCALE_ROWS = K_PASS // 32
 LEAD_LOADS = 2 * CHUNKS
-LEAD_ROWS = SCALE_ROWS // LEAD_LOADS
+LEAD_PAIRS = SCALE_ROWS // 2 // LEAD_LOADS
+assert SCALE_ROWS // 2 == ROUNDS
 
 FLOPS = 2 * ROWS * FEATURES * WINDOWS * WINDOW_K
 
 
-def load_scale_row(nc, w_planes, scales, q):
-    first = QUADRANT * (q // PLANE_ROWS) + q % PLANE_ROWS
-    nc.sync.dma_start(
-        out=w_planes[first : first + PLANE_ROWS * WINDOWS : PLANE_ROWS, :]
-        .bitcast(I32)
-        .rearrange("w (g h) -> w g h", g=PASSES),
-        in_=scales.rearrange("(w g) q h -> q w g h", w=WINDOWS)[q].bitcast(I32),
-    )
+def zeroed_planes(nc, keep, w):
+    w_planes = keep.tile([P, PASSES * FEATURES], U8, name="w_planes%d" % w, align_bytes=64)
+    nc.vector.memset(w_planes[:].bitcast(I32), 0)
+    return w_planes
+
+
+def load_scale_pair(nc, w_planes, scales, w, i):
+    for q in (i, i + SCALE_ROWS // 2):
+        p = QUADRANT * (q // PLANE_ROWS) + PLANE_ROWS * w + q % PLANE_ROWS
+        nc.sync.dma_start(
+            out=w_planes[p : p + 1, :].bitcast(I32).rearrange("o (g h) -> o g h", g=PASSES),
+            in_=scales[w * PASSES : (w + 1) * PASSES, q : q + 1, :].rearrange("g o h -> o g h").bitcast(I32),
+        )
 
 
 def load_x_window(nc, x_pool, x, w, w_planes, scales):
@@ -59,12 +65,12 @@ def load_x_window(nc, x_pool, x, w, w_planes, scales):
         x_chunks.append(x_chunk)
         lead = w * CHUNKS + c
         if lead < LEAD_LOADS:
-            for q in range(lead * LEAD_ROWS, (lead + 1) * LEAD_ROWS):
-                load_scale_row(nc, w_planes, scales, q)
+            for i in range(lead * LEAD_PAIRS, (lead + 1) * LEAD_PAIRS):
+                load_scale_pair(nc, w_planes[0], scales, 0, i)
     return x_chunks
 
 
-def load_weight_window(nc, w_pool, words, w):
+def load_weight_window(nc, w_pool, words, w, w_planes, scales):
     w_rounds = []
     for r in range(ROUNDS):
         first_pass = w * PASSES + r * ROUND
@@ -74,6 +80,8 @@ def load_weight_window(nc, w_pool, words, w):
             in_=words[first_pass : first_pass + ROUND].rearrange("g p h t -> p g (h t)").bitcast(I32),
         )
         w_rounds.append(w_round)
+        if w + 1 < WINDOWS:
+            load_scale_pair(nc, w_planes[w + 1], scales, w + 1, r)
     return w_rounds
 
 
@@ -165,8 +173,7 @@ def tile_dendriticlayersilu_ffn_k_kernel(tc, x, template_flat_words, template_fl
 
         ident = keep.tile([P, P], F32)
         make_identity(nc, ident[:])
-        w_planes = keep.tile([P, PASSES * FEATURES], U8, align_bytes=64)
-        nc.vector.memset(w_planes[:].bitcast(I32), 0)
+        w_planes = [zeroed_planes(nc, keep, w) for w in range(WINDOWS)]
 
         lse = keep.tile([P, FEATURES], F32)
         avg = keep.tile([P, FEATURES], F32)
@@ -177,11 +184,11 @@ def tile_dendriticlayersilu_ffn_k_kernel(tc, x, template_flat_words, template_fl
             x_codes, x_planes = ahead
             if w + 1 < WINDOWS:
                 x_chunks = load_x_window(nc, x_pool, x, w + 1, w_planes, template_flat_scales)
-            w_rounds = load_weight_window(nc, w_pool, template_flat_words, w)
+            w_rounds = load_weight_window(nc, w_pool, template_flat_words, w, w_planes, template_flat_scales)
             if w + 1 < WINDOWS:
                 ahead = quantise_x_window(nc, code_pool, grouped_pool, bank_pool, ident, x_chunks)
             score = score_pool.tile([P, FEATURES], F32)
-            score_window(nc, score, x_codes, x_planes, w_rounds, w_planes, w)
+            score_window(nc, score, x_codes, x_planes, w_rounds, w_planes[w], w)
             fold_window(nc, work, lse, avg, score, w)
 
         nc.sync.dma_start(out=out[:, :], in_=avg[:])

@@ -31,6 +31,7 @@ VECTOR_EVERY = 4
 CHUNK = 16
 CHUNK_ROUNDS = CHUNK // ROUND
 CHUNKS = PASSES // CHUNK
+LOAD_ALIGN = 1024
 QUADRANT = 32
 PLANE_ROWS = 4
 SCALE_ROWS = K_PASS // 32
@@ -42,7 +43,7 @@ FLOPS = 2 * ROWS * FEATURES * WINDOWS * WINDOW_K
 
 
 def zeroed_planes(nc, keep, w):
-    w_planes = keep.tile([P, PASSES * FEATURES], U8, name="w_planes%d" % w, align_bytes=64)
+    w_planes = keep.tile([P, PASSES * FEATURES], U8, name="w_planes%d" % w, align_bytes=LOAD_ALIGN)
     nc.vector.memset(w_planes[:].bitcast(I32), 0)
     return w_planes
 
@@ -60,7 +61,7 @@ def load_x_window(nc, x_pool, x, w, w_planes, scales):
     x_chunks = []
     for c in range(CHUNKS):
         first_k = w * WINDOW_K + c * CHUNK * K_PASS
-        x_chunk = x_pool.tile([P, CHUNK * K_PASS], BF16)
+        x_chunk = x_pool.tile([P, CHUNK * K_PASS], BF16, align_bytes=LOAD_ALIGN)
         nc.sync.dma_start(out=x_chunk[:], in_=x[:, first_k : first_k + CHUNK * K_PASS])
         x_chunks.append(x_chunk)
         lead = w * CHUNKS + c
@@ -74,7 +75,7 @@ def load_weight_window(nc, w_pool, words, w, w_planes, scales):
     w_rounds = []
     for r in range(ROUNDS):
         first_pass = w * PASSES + r * ROUND
-        w_round = w_pool.tile([P, ROUND, FEATURES], U32, align_bytes=64)
+        w_round = w_pool.tile([P, ROUND, FEATURES], U32, align_bytes=LOAD_ALIGN)
         nc.sync.dma_start(
             out=w_round[:].bitcast(I32),
             in_=words[first_pass : first_pass + ROUND].rearrange("g p h t -> p g (h t)").bitcast(I32),

@@ -25,6 +25,8 @@ PASS_WORDS = K_PASS // PAIR
 
 ROUND = 4
 ROUNDS = PASSES // ROUND
+W_LOAD = 8
+LAST_LOADS = (8, 8, 8, 4, 4)
 BANK_PASSES = 2
 BANKS = ROUND // BANK_PASSES
 VECTOR_EVERY = 4
@@ -37,7 +39,7 @@ PLANE_ROWS = 4
 SCALE_ROWS = K_PASS // 32
 LEAD_LOADS = 2 * CHUNKS
 LEAD_PAIRS = SCALE_ROWS // 2 // LEAD_LOADS
-assert SCALE_ROWS // 2 == ROUNDS
+W_PAIRS = SCALE_ROWS // 2 * W_LOAD // PASSES
 
 FLOPS = 2 * ROWS * FEATURES * WINDOWS * WINDOW_K
 
@@ -72,18 +74,19 @@ def load_x_window(nc, x_pool, x, w, w_planes, scales):
 
 
 def load_weight_window(nc, w_pool, words, w, w_planes, scales):
-    w_rounds = []
-    for r in range(ROUNDS):
-        first_pass = w * PASSES + r * ROUND
-        w_round = w_pool.tile([P, ROUND, FEATURES], U32, align_bytes=LOAD_ALIGN)
+    w_passes = []
+    for i, count in enumerate(LAST_LOADS if w == WINDOWS - 1 else (W_LOAD,) * (PASSES // W_LOAD)):
+        first_pass = w * PASSES + len(w_passes)
+        w_load = w_pool.tile([P, W_LOAD, FEATURES], U32, align_bytes=LOAD_ALIGN)
         nc.sync.dma_start(
-            out=w_round[:].bitcast(I32),
-            in_=words[first_pass : first_pass + ROUND].rearrange("g p h t -> p g (h t)").bitcast(I32),
+            out=w_load[:, :count, :].bitcast(I32),
+            in_=words[first_pass : first_pass + count].rearrange("g p h t -> p g (h t)").bitcast(I32),
         )
-        w_rounds.append(w_round)
+        w_passes.extend((w_load, g) for g in range(count))
         if w + 1 < WINDOWS:
-            load_scale_pair(nc, w_planes[w + 1], scales, w + 1, r)
-    return w_rounds
+            for pair in range(i * W_PAIRS, (i + 1) * W_PAIRS):
+                load_scale_pair(nc, w_planes[w + 1], scales, w + 1, pair)
+    return w_passes
 
 
 def quantise_x_window(nc, code_pool, grouped_pool, bank_pool, ident, x_chunks):
@@ -121,14 +124,15 @@ def quantise_x_window(nc, code_pool, grouped_pool, bank_pool, ident, x_chunks):
     return x_codes, x_planes
 
 
-def score_window(nc, score, x_codes, x_planes, w_rounds, w_planes, w):
+def score_window(nc, score, x_codes, x_planes, w_passes, w_planes, w):
     for g in range(PASSES):
         rows = slice(g * ROWS, (g + 1) * ROWS)
+        w_load, place = w_passes[g]
         nc.tensor.matmul_mx(
             out=score[:],
             lhsT=x_codes[:, rows].bitcast(FP8X4),
             lhsT_scale=x_planes[:, rows],
-            rhs=w_rounds[g // ROUND][:, g % ROUND, :].bitcast(FP8X4),
+            rhs=w_load[:, place, :].bitcast(FP8X4),
             rhs_scale=w_planes[PLANE_ROWS * w : P, g * FEATURES : (g + 1) * FEATURES],
             start=(g == 0),
             stop=(g == PASSES - 1),
@@ -164,7 +168,7 @@ def tile_dendriticlayersilu_ffn_k_kernel(tc, x, template_flat_words, template_fl
     with ExitStack() as ctx:
         keep = ctx.enter_context(tc.tile_pool(name="keep", bufs=1))
         x_pool = ctx.enter_context(tc.tile_pool(name="x", bufs=2 * CHUNKS))
-        w_pool = ctx.enter_context(tc.tile_pool(name="w", bufs=2 * ROUNDS))
+        w_pool = ctx.enter_context(tc.tile_pool(name="w", bufs=2 * PASSES // W_LOAD))
         code_pool = ctx.enter_context(tc.tile_pool(name="codes", bufs=2))
         grouped_pool = ctx.enter_context(tc.tile_pool(name="grouped", bufs=3))
         work = ctx.enter_context(tc.tile_pool(name="work", bufs=2))
@@ -185,11 +189,11 @@ def tile_dendriticlayersilu_ffn_k_kernel(tc, x, template_flat_words, template_fl
             x_codes, x_planes = ahead
             if w + 1 < WINDOWS:
                 x_chunks = load_x_window(nc, x_pool, x, w + 1, w_planes, template_flat_scales)
-            w_rounds = load_weight_window(nc, w_pool, template_flat_words, w, w_planes, template_flat_scales)
+            w_passes = load_weight_window(nc, w_pool, template_flat_words, w, w_planes, template_flat_scales)
             if w + 1 < WINDOWS:
                 ahead = quantise_x_window(nc, code_pool, grouped_pool, bank_pool, ident, x_chunks)
             score = score_pool.tile([P, FEATURES], F32)
-            score_window(nc, score, x_codes, x_planes, w_rounds, w_planes[w], w)
+            score_window(nc, score, x_codes, x_planes, w_passes, w_planes[w], w)
             fold_window(nc, work, lse, avg, score, w)
 
         nc.sync.dma_start(out=out[:, :], in_=avg[:])

@@ -37,45 +37,50 @@ LOAD_ALIGN = 1024
 QUADRANT = 32
 PLANE_ROWS = 4
 SCALE_ROWS = K_PASS // 32
-LEAD_LOADS = 2 * CHUNKS
-LEAD_PAIRS = SCALE_ROWS // 2 // LEAD_LOADS
-W_PAIRS = SCALE_ROWS // 2 * W_LOAD // PASSES
+TILE_WINDOWS = 2
+PAIRS = SCALE_ROWS // 2
 
 FLOPS = 2 * ROWS * FEATURES * WINDOWS * WINDOW_K
 
 
-def zeroed_planes(nc, keep, w):
-    w_planes = keep.tile([P, PASSES * FEATURES], U8, name="w_planes%d" % w, align_bytes=LOAD_ALIGN)
+def zeroed_planes(nc, keep, t):
+    w_planes = keep.tile([P, PASSES * FEATURES], U8, name="w_planes%d" % t, align_bytes=LOAD_ALIGN)
     nc.vector.memset(w_planes[:].bitcast(I32), 0)
     return w_planes
 
 
-def load_scale_pair(nc, w_planes, scales, w, i):
-    for q in (i, i + SCALE_ROWS // 2):
-        p = QUADRANT * (q // PLANE_ROWS) + PLANE_ROWS * w + q % PLANE_ROWS
-        nc.sync.dma_start(
-            out=w_planes[p : p + 1, :].bitcast(I32).rearrange("o (g h) -> o g h", g=PASSES),
-            in_=scales[w * PASSES : (w + 1) * PASSES, q : q + 1, :].rearrange("g o h -> o g h").bitcast(I32),
-        )
+def load_scale_row(nc, w_planes, scales, w, q):
+    p = QUADRANT * (q // PLANE_ROWS) + PLANE_ROWS * w + q % PLANE_ROWS
+    nc.sync.dma_start(
+        out=w_planes[w // TILE_WINDOWS][p : p + 1, :].bitcast(I32).rearrange("o (g h) -> o g h", g=PASSES),
+        in_=scales[w * PASSES : (w + 1) * PASSES, q : q + 1, :].rearrange("g o h -> o g h").bitcast(I32),
+    )
 
 
-def load_x_window(nc, x_pool, x, w, w_planes, scales):
+def load_scale_burst(nc, w_planes, scales, burst):
+    first_w = TILE_WINDOWS * (burst // PAIRS)
+    i = burst % PAIRS
+    for half in (0, PAIRS):
+        load_scale_row(nc, w_planes, scales, first_w, i + half)
+        load_scale_row(nc, w_planes, scales, first_w + 1, (i + PAIRS // 2) % PAIRS + half)
+
+
+def load_x_window(nc, x_pool, x, w, w_planes, scales, bursts):
     x_chunks = []
     for c in range(CHUNKS):
         first_k = w * WINDOW_K + c * CHUNK * K_PASS
         x_chunk = x_pool.tile([P, CHUNK * K_PASS], BF16, align_bytes=LOAD_ALIGN)
         nc.sync.dma_start(out=x_chunk[:], in_=x[:, first_k : first_k + CHUNK * K_PASS])
         x_chunks.append(x_chunk)
-        lead = w * CHUNKS + c
-        if lead < LEAD_LOADS:
-            for i in range(lead * LEAD_PAIRS, (lead + 1) * LEAD_PAIRS):
-                load_scale_pair(nc, w_planes[0], scales, 0, i)
+        if bursts:
+            load_scale_burst(nc, w_planes, scales, bursts[0])
+            bursts.remove(bursts[0])
     return x_chunks
 
 
-def load_weight_window(nc, w_pool, words, w, w_planes, scales):
+def load_weight_window(nc, w_pool, words, w, w_planes, scales, bursts):
     w_passes = []
-    for i, count in enumerate(LAST_LOADS if w == WINDOWS - 1 else (W_LOAD,) * (PASSES // W_LOAD)):
+    for count in LAST_LOADS if w == WINDOWS - 1 else (W_LOAD,) * (PASSES // W_LOAD):
         first_pass = w * PASSES + len(w_passes)
         w_load = w_pool.tile([P, W_LOAD, FEATURES], U32, align_bytes=LOAD_ALIGN)
         nc.sync.dma_start(
@@ -83,9 +88,9 @@ def load_weight_window(nc, w_pool, words, w, w_planes, scales):
             in_=words[first_pass : first_pass + count].rearrange("g p h t -> p g (h t)").bitcast(I32),
         )
         w_passes.extend((w_load, g) for g in range(count))
-        if w + 1 < WINDOWS:
-            for pair in range(i * W_PAIRS, (i + 1) * W_PAIRS):
-                load_scale_pair(nc, w_planes[w + 1], scales, w + 1, pair)
+        if bursts:
+            load_scale_burst(nc, w_planes, scales, bursts[0])
+            bursts.remove(bursts[0])
     return w_passes
 
 
@@ -178,22 +183,23 @@ def tile_dendriticlayersilu_ffn_k_kernel(tc, x, template_flat_words, template_fl
 
         ident = keep.tile([P, P], F32)
         make_identity(nc, ident[:])
-        w_planes = [zeroed_planes(nc, keep, w) for w in range(WINDOWS)]
+        w_planes = [zeroed_planes(nc, keep, t) for t in range(WINDOWS // TILE_WINDOWS)]
 
         lse = keep.tile([P, FEATURES], F32)
         avg = keep.tile([P, FEATURES], F32)
 
-        x_chunks = load_x_window(nc, x_pool, x, 0, w_planes, template_flat_scales)
+        bursts = list(range(WINDOWS * SCALE_ROWS // 4))
+        x_chunks = load_x_window(nc, x_pool, x, 0, w_planes, template_flat_scales, bursts)
         ahead = quantise_x_window(nc, code_pool, grouped_pool, bank_pool, ident, x_chunks)
         for w in range(WINDOWS):
             x_codes, x_planes = ahead
             if w + 1 < WINDOWS:
-                x_chunks = load_x_window(nc, x_pool, x, w + 1, w_planes, template_flat_scales)
-            w_passes = load_weight_window(nc, w_pool, template_flat_words, w, w_planes, template_flat_scales)
+                x_chunks = load_x_window(nc, x_pool, x, w + 1, w_planes, template_flat_scales, bursts)
+            w_passes = load_weight_window(nc, w_pool, template_flat_words, w, w_planes, template_flat_scales, bursts)
             if w + 1 < WINDOWS:
                 ahead = quantise_x_window(nc, code_pool, grouped_pool, bank_pool, ident, x_chunks)
             score = score_pool.tile([P, FEATURES], F32)
-            score_window(nc, score, x_codes, x_planes, w_passes, w_planes[w], w)
+            score_window(nc, score, x_codes, x_planes, w_passes, w_planes[w // TILE_WINDOWS], w)
             fold_window(nc, work, lse, avg, score, w)
 
         nc.sync.dma_start(out=out[:, :], in_=avg[:])

@@ -15,6 +15,7 @@ ALU = mybir.AluOpType
 P = 128
 ROWS = 128
 FEATURES = 256
+HALVES = (slice(0, FEATURES // 2), slice(FEATURES // 2, FEATURES))
 WINDOWS = 4
 WINDOW_K = 16384
 PACK = 4
@@ -25,8 +26,8 @@ PASS_WORDS = K_PASS // PAIR
 
 ROUND = 4
 ROUNDS = PASSES // ROUND
-W_LOAD = 8
-LAST_LOADS = (8, 8, 8, 4, 4)
+W_LOAD = 16
+W_LOADS = ((8, 8, 8, 8), (16, 16), (16, 16), (16, 8, 4, 4))
 BANK_PASSES = 2
 BANKS = ROUND // BANK_PASSES
 VECTOR_EVERY = 4
@@ -57,12 +58,21 @@ def load_scale_row(nc, w_planes, scales, w, q):
     )
 
 
-def load_scale_burst(nc, w_planes, scales, burst):
-    first_w = TILE_WINDOWS * (burst // PAIRS)
-    i = burst % PAIRS
-    for half in (0, PAIRS):
-        load_scale_row(nc, w_planes, scales, first_w, i + half)
-        load_scale_row(nc, w_planes, scales, first_w + 1, (i + PAIRS // 2) % PAIRS + half)
+def scale_bursts():
+    pairs = [(2, i // 2) if i % 2 == 0 else (3, i // 2) for i in range(2 * PAIRS)]
+    first = [[(0, i), (1, (i + PAIRS // 2) % PAIRS)] for i in range(PAIRS)]
+    for burst in first[1:]:
+        burst.append(pairs[0])
+        pairs.remove(pairs[0])
+    rest = [pairs[i : i + 2] for i in range(0, len(pairs), 2)]
+    return [[(w, i + half) for half in (0, PAIRS) for w, i in burst] for burst in first + rest]
+
+
+def load_scale_burst(nc, w_planes, scales, bursts):
+    if bursts:
+        for w, q in bursts[0]:
+            load_scale_row(nc, w_planes, scales, w, q)
+        bursts.remove(bursts[0])
 
 
 def load_x_window(nc, x_pool, x, w, w_planes, scales, bursts):
@@ -72,15 +82,13 @@ def load_x_window(nc, x_pool, x, w, w_planes, scales, bursts):
         x_chunk = x_pool.tile([P, CHUNK * K_PASS], BF16, align_bytes=LOAD_ALIGN)
         nc.sync.dma_start(out=x_chunk[:], in_=x[:, first_k : first_k + CHUNK * K_PASS])
         x_chunks.append(x_chunk)
-        if bursts:
-            load_scale_burst(nc, w_planes, scales, bursts[0])
-            bursts.remove(bursts[0])
+        load_scale_burst(nc, w_planes, scales, bursts)
     return x_chunks
 
 
 def load_weight_window(nc, w_pool, words, w, w_planes, scales, bursts):
     w_passes = []
-    for count in LAST_LOADS if w == WINDOWS - 1 else (W_LOAD,) * (PASSES // W_LOAD):
+    for count in W_LOADS[w]:
         first_pass = w * PASSES + len(w_passes)
         w_load = w_pool.tile([P, W_LOAD, FEATURES], U32, align_bytes=LOAD_ALIGN)
         nc.sync.dma_start(
@@ -88,9 +96,7 @@ def load_weight_window(nc, w_pool, words, w, w_planes, scales, bursts):
             in_=words[first_pass : first_pass + count].rearrange("g p h t -> p g (h t)").bitcast(I32),
         )
         w_passes.extend((w_load, g) for g in range(count))
-        if bursts:
-            load_scale_burst(nc, w_planes, scales, bursts[0])
-            bursts.remove(bursts[0])
+        load_scale_burst(nc, w_planes, scales, bursts)
     return w_passes
 
 
@@ -153,12 +159,18 @@ def fold_window(nc, work, lse, avg, score, w):
         return
     share = work.tile([P, FEATURES], F32)
     step = work.tile([P, FEATURES], F32)
-    nc.vector.tensor_sub(out=share[:], in0=score[:], in1=lse[:])
-    nc.scalar.activation(out=share[:], in_=share[:], func=ACT.Sigmoid)
-    nc.vector.tensor_mul(out=step[:], in0=score[:], in1=sig[:])
-    nc.vector.tensor_sub(out=step[:], in0=step[:], in1=avg[:])
-    nc.vector.tensor_mul(out=step[:], in0=step[:], in1=share[:])
-    nc.vector.tensor_add(out=avg[:], in0=avg[:], in1=step[:])
+    for cols in HALVES:
+        nc.vector.tensor_sub(out=share[:, cols], in0=score[:, cols], in1=lse[:, cols])
+    for cols in HALVES:
+        nc.scalar.activation(out=share[:, cols], in_=share[:, cols], func=ACT.Sigmoid)
+    for cols in HALVES:
+        nc.vector.tensor_mul(out=step[:, cols], in0=score[:, cols], in1=sig[:, cols])
+    for cols in HALVES:
+        nc.vector.tensor_sub(out=step[:, cols], in0=step[:, cols], in1=avg[:, cols])
+    for cols in HALVES:
+        nc.vector.tensor_mul(out=step[:, cols], in0=step[:, cols], in1=share[:, cols])
+    for cols in HALVES:
+        nc.vector.tensor_add(out=avg[:, cols], in0=avg[:, cols], in1=step[:, cols])
     if w < WINDOWS - 1:
         larger = work.tile([P, FEATURES], F32)
         nc.vector.tensor_max(out=lse[:], in0=score[:], in1=lse[:])
@@ -173,7 +185,7 @@ def tile_dendriticlayersilu_ffn_k_kernel(tc, x, template_flat_words, template_fl
     with ExitStack() as ctx:
         keep = ctx.enter_context(tc.tile_pool(name="keep", bufs=1))
         x_pool = ctx.enter_context(tc.tile_pool(name="x", bufs=2 * CHUNKS))
-        w_pool = ctx.enter_context(tc.tile_pool(name="w", bufs=2 * PASSES // W_LOAD))
+        w_pool = ctx.enter_context(tc.tile_pool(name="w", bufs=2 * PASSES // W_LOAD + 1))
         code_pool = ctx.enter_context(tc.tile_pool(name="codes", bufs=2))
         grouped_pool = ctx.enter_context(tc.tile_pool(name="grouped", bufs=3))
         work = ctx.enter_context(tc.tile_pool(name="work", bufs=2))
@@ -188,7 +200,7 @@ def tile_dendriticlayersilu_ffn_k_kernel(tc, x, template_flat_words, template_fl
         lse = keep.tile([P, FEATURES], F32)
         avg = keep.tile([P, FEATURES], F32)
 
-        bursts = list(range(WINDOWS * SCALE_ROWS // 4))
+        bursts = scale_bursts()
         x_chunks = load_x_window(nc, x_pool, x, 0, w_planes, template_flat_scales, bursts)
         ahead = quantise_x_window(nc, code_pool, grouped_pool, bank_pool, ident, x_chunks)
         for w in range(WINDOWS):
@@ -202,4 +214,5 @@ def tile_dendriticlayersilu_ffn_k_kernel(tc, x, template_flat_words, template_fl
             score_window(nc, score, x_codes, x_planes, w_passes, w_planes[w // TILE_WINDOWS], w)
             fold_window(nc, work, lse, avg, score, w)
 
-        nc.sync.dma_start(out=out[:, :], in_=avg[:])
+        for cols in HALVES:
+            nc.sync.dma_start(out=out[:, cols], in_=avg[:, cols])

@@ -27,7 +27,7 @@ PASS_WORDS = K_PASS // PAIR
 ROUND = 4
 ROUNDS = PASSES // ROUND
 W_LOAD = 16
-W_LOADS = ((8, 8, 8, 8), (16, 16), (16, 16), (16, 8, 4, 4))
+W_LOADS = ((16, 16), (16, 16), (16, 16), (16, 8, 4, 4))
 BANK_PASSES = 2
 BANKS = ROUND // BANK_PASSES
 VECTOR_EVERY = 4
@@ -185,8 +185,8 @@ def tile_dendriticlayersilu_ffn_k_kernel(tc, x, template_flat_words, template_fl
     with ExitStack() as ctx:
         keep = ctx.enter_context(tc.tile_pool(name="keep", bufs=1))
         x_pool = ctx.enter_context(tc.tile_pool(name="x", bufs=2 * CHUNKS))
-        w_pool = ctx.enter_context(tc.tile_pool(name="w", bufs=2 * PASSES // W_LOAD + 1))
-        code_pool = ctx.enter_context(tc.tile_pool(name="codes", bufs=2))
+        w_pool = ctx.enter_context(tc.tile_pool(name="w", bufs=2 * PASSES // W_LOAD))
+        code_pool = ctx.enter_context(tc.tile_pool(name="codes", bufs=3))
         grouped_pool = ctx.enter_context(tc.tile_pool(name="grouped", bufs=3))
         work = ctx.enter_context(tc.tile_pool(name="work", bufs=2))
         score_pool = ctx.enter_context(tc.psum_pool(name="score", bufs=2))
@@ -201,18 +201,37 @@ def tile_dendriticlayersilu_ffn_k_kernel(tc, x, template_flat_words, template_fl
         avg = keep.tile([P, FEATURES], F32)
 
         bursts = scale_bursts()
-        x_chunks = load_x_window(nc, x_pool, x, 0, w_planes, template_flat_scales, bursts)
-        ahead = quantise_x_window(nc, code_pool, grouped_pool, bank_pool, ident, x_chunks)
-        for w in range(WINDOWS):
-            x_codes, x_planes = ahead
-            if w + 1 < WINDOWS:
-                x_chunks = load_x_window(nc, x_pool, x, w + 1, w_planes, template_flat_scales, bursts)
-            w_passes = load_weight_window(nc, w_pool, template_flat_words, w, w_planes, template_flat_scales, bursts)
-            if w + 1 < WINDOWS:
-                ahead = quantise_x_window(nc, code_pool, grouped_pool, bank_pool, ident, x_chunks)
-            score = score_pool.tile([P, FEATURES], F32)
-            score_window(nc, score, x_codes, x_planes, w_passes, w_planes[w // TILE_WINDOWS], w)
+
+        def load_x(w):
+            return load_x_window(nc, x_pool, x, w, w_planes, template_flat_scales, bursts)
+
+        def load_weights(w):
+            return load_weight_window(nc, w_pool, template_flat_words, w, w_planes, template_flat_scales, bursts)
+
+        def quantise(x_chunks):
+            return quantise_x_window(nc, code_pool, grouped_pool, bank_pool, ident, x_chunks)
+
+        def take_in(w, quantised, w_passes):
+            score = score_pool.tile([P, FEATURES], F32, name="score")
+            score_window(nc, score, quantised[0], quantised[1], w_passes, w_planes[w // TILE_WINDOWS], w)
             fold_window(nc, work, lse, avg, score, w)
+
+        x_0 = load_x(0)
+        quantised_0 = quantise(x_0)
+        x_1 = load_x(1)
+        weights_0 = load_weights(0)
+        x_2 = load_x(2)
+        quantised_1 = quantise(x_1)
+        quantised_2 = quantise(x_2)
+        take_in(0, quantised_0, weights_0)
+        weights_1 = load_weights(1)
+        take_in(1, quantised_1, weights_1)
+        x_3 = load_x(3)
+        quantised_3 = quantise(x_3)
+        weights_2 = load_weights(2)
+        take_in(2, quantised_2, weights_2)
+        weights_3 = load_weights(3)
+        take_in(3, quantised_3, weights_3)
 
         for cols in HALVES:
             nc.sync.dma_start(out=out[:, cols], in_=avg[:, cols])

from contextlib import ExitStack

import concourse.mybir as mybir
from concourse.masks import make_identity

F32 = mybir.dt.float32
BF16 = mybir.dt.bfloat16
I32 = mybir.dt.int32
U32 = mybir.dt.uint32
U8 = mybir.dt.uint8
FP8X4 = mybir.dt.float8_e4m3fn_x4
ACT = mybir.ActivationFunctionType
ALU = mybir.AluOpType

P = 128
ROWS = 128
FEATURES = 256
HALVES = (slice(0, FEATURES // 2), slice(FEATURES // 2, FEATURES))
WINDOWS = 4
WINDOW_K = 16384
PACK = 4
K_PASS = P * PACK
PASSES = WINDOW_K // K_PASS
PAIR = 2
PASS_WORDS = K_PASS // PAIR

ROUND = 4
ROUNDS = PASSES // ROUND
W_LOAD = 16
W_LOADS = ((16, 16), (16, 16), (16, 16), (16, 8, 4, 4))
BANK_PASSES = 2
BANKS = ROUND // BANK_PASSES
VECTOR_EVERY = 4
CHUNK = 16
CHUNK_ROUNDS = CHUNK // ROUND
CHUNKS = PASSES // CHUNK
LOAD_ALIGN = 1024
QUADRANT = 32
PLANE_ROWS = 4
SCALE_ROWS = K_PASS // 32
TILE_WINDOWS = 2
PAIRS = SCALE_ROWS // 2

FLOPS = 2 * ROWS * FEATURES * WINDOWS * WINDOW_K


def zeroed_planes(nc, keep, t):
    w_planes = keep.tile([P, PASSES * FEATURES], U8, name="w_planes%d" % t, align_bytes=LOAD_ALIGN)
    nc.vector.memset(w_planes[:].bitcast(I32), 0)
    return w_planes


def load_scale_row(nc, w_planes, scales, w, q):
    p = QUADRANT * (q // PLANE_ROWS) + PLANE_ROWS * w + q % PLANE_ROWS
    nc.sync.dma_start(
        out=w_planes[w // TILE_WINDOWS][p : p + 1, :].bitcast(I32).rearrange("o (g h) -> o g h", g=PASSES),
        in_=scales[w * PASSES : (w + 1) * PASSES, q : q + 1, :].rearrange("g o h -> o g h").bitcast(I32),
    )


def scale_bursts():
    pairs = [(2, i // 2) if i % 2 == 0 else (3, i // 2) for i in range(2 * PAIRS)]
    first = [[(0, i), (1, (i + PAIRS // 2) % PAIRS)] for i in range(PAIRS)]
    for burst in first[1:]:
        burst.append(pairs[0])
        pairs.remove(pairs[0])
    rest = [pairs[i : i + 2] for i in range(0, len(pairs), 2)]
    return [[(w, i + half) for half in (0, PAIRS) for w, i in burst] for burst in first + rest]


def load_scale_burst(nc, w_planes, scales, bursts):
    if bursts:
        for w, q in bursts[0]:
            load_scale_row(nc, w_planes, scales, w, q)
        bursts.remove(bursts[0])


def load_x_window(nc, x_pool, x, w, w_planes, scales, bursts):
    x_chunks = []
    for c in range(CHUNKS):
        first_k = w * WINDOW_K + c * CHUNK * K_PASS
        x_chunk = x_pool.tile([P, CHUNK * K_PASS], BF16, align_bytes=LOAD_ALIGN)
        nc.sync.dma_start(out=x_chunk[:], in_=x[:, first_k : first_k + CHUNK * K_PASS])
        x_chunks.append(x_chunk)
        load_scale_burst(nc, w_planes, scales, bursts)
    return x_chunks


def load_weight_window(nc, w_pool, words, w, w_planes, scales, bursts):
    w_passes = []
    for count in W_LOADS[w]:
        first_pass = w * PASSES + len(w_passes)
        w_load = w_pool.tile([P, W_LOAD, FEATURES], U32, align_bytes=LOAD_ALIGN)
        nc.sync.dma_start(
            out=w_load[:, :count, :].bitcast(I32),
            in_=words[first_pass : first_pass + count].rearrange("g p h t -> p g (h t)").bitcast(I32),
        )
        w_passes.extend((w_load, g) for g in range(count))
        load_scale_burst(nc, w_planes, scales, bursts)
    return w_passes


def quantise_x_window(nc, code_pool, grouped_pool, bank_pool, ident, x_chunks):
    x_codes = code_pool.tile([P, PASSES * ROWS], U32, align_bytes=64)
    x_planes = code_pool.tile([P, PASSES * ROWS], U8, align_bytes=64)

    def quantise_round(r, grouped):
        cols = slice(r * ROUND * ROWS, (r + 1) * ROUND * ROWS)
        nc.vector.quantize_mx(out=x_codes[:, cols].bitcast(FP8X4), scales=x_planes[:, cols], in_=grouped[:])

    earlier = None
    for r in range(ROUNDS):
        x_words = x_chunks[r // CHUNK_ROUNDS][:].bitcast(F32)
        grouped = grouped_pool.tile([P, ROUND * ROWS * PACK], BF16, align_bytes=64)
        grouped_words = grouped[:].bitcast(F32).rearrange("p (a n u) -> p a n u", n=ROWS, u=PAIR)
        for b in range(BANKS):
            bank = bank_pool.tile([P, BANK_PASSES, PAIR, ROWS], F32)
            for a in range(BANK_PASSES):
                first_word = ((r % CHUNK_ROUNDS) * ROUND + b * BANK_PASSES + a) * PASS_WORDS
                for u in range(PAIR):
                    nc.tensor.transpose(
                        out=bank[:, a, u, :],
                        in_=x_words[:, first_word + u : first_word + PASS_WORDS : PAIR],
                        identity=ident[:],
                    )
            passes = slice(b * BANK_PASSES, (b + 1) * BANK_PASSES)
            if (r * BANKS + b) % VECTOR_EVERY == VECTOR_EVERY - 1:
                nc.vector.tensor_copy(out=grouped_words[:, passes], in_=bank[:].rearrange("p a u n -> p a n u"))
            else:
                nc.scalar.copy(out=grouped_words[:, passes], in_=bank[:].rearrange("p a u n -> p a n u"))
        if r > 0:
            quantise_round(r - 1, earlier)
        earlier = grouped
    quantise_round(ROUNDS - 1, earlier)
    return x_codes, x_planes


def score_window(nc, score, x_codes, x_planes, w_passes, w_planes, w):
    for g in range(PASSES):
        rows = slice(g * ROWS, (g + 1) * ROWS)
        w_load, place = w_passes[g]
        nc.tensor.matmul_mx(
            out=score[:],
            lhsT=x_codes[:, rows].bitcast(FP8X4),
            lhsT_scale=x_planes[:, rows],
            rhs=w_load[:, place, :].bitcast(FP8X4),
            rhs_scale=w_planes[PLANE_ROWS * w : P, g * FEATURES : (g + 1) * FEATURES],
            start=(g == 0),
            stop=(g == PASSES - 1),
        )


def fold_window(nc, work, lse, avg, score, w):
    sig = work.tile([P, FEATURES], F32)
    nc.scalar.activation(out=sig[:], in_=score[:], func=ACT.Sigmoid)
    if w == 0:
        nc.vector.tensor_copy(out=lse[:], in_=score[:])
        nc.vector.tensor_mul(out=avg[:], in0=lse[:], in1=sig[:])
        return
    share = work.tile([P, FEATURES], F32)
    step = work.tile([P, FEATURES], F32)
    for cols in HALVES:
        nc.vector.tensor_sub(out=share[:, cols], in0=score[:, cols], in1=lse[:, cols])
    for cols in HALVES:
        nc.scalar.activation(out=share[:, cols], in_=share[:, cols], func=ACT.Sigmoid)
    for cols in HALVES:
        nc.vector.tensor_mul(out=step[:, cols], in0=score[:, cols], in1=sig[:, cols])
    for cols in HALVES:
        nc.vector.tensor_sub(out=step[:, cols], in0=step[:, cols], in1=avg[:, cols])
    for cols in HALVES:
        nc.vector.tensor_mul(out=step[:, cols], in0=step[:, cols], in1=share[:, cols])
    for cols in HALVES:
        nc.vector.tensor_add(out=avg[:, cols], in0=avg[:, cols], in1=step[:, cols])
    if w < WINDOWS - 1:
        larger = work.tile([P, FEATURES], F32)
        nc.vector.tensor_max(out=lse[:], in0=score[:], in1=lse[:])
        nc.vector.tensor_scalar(out=larger[:], in0=share[:], scalar1=-1.0, scalar2=1.0, op0=ALU.mult, op1=ALU.add)
        nc.vector.tensor_max(out=larger[:], in0=larger[:], in1=share[:])
        nc.scalar.activation(out=larger[:], in_=larger[:], func=ACT.Ln)
        nc.vector.tensor_sub(out=lse[:], in0=lse[:], in1=larger[:])


def tile_dendriticlayersilu_ffn_k_kernel(tc, x, template_flat_words, template_flat_scales, out):
    nc = tc.nc
    with ExitStack() as ctx:
        keep = ctx.enter_context(tc.tile_pool(name="keep", bufs=1))
        x_pool = ctx.enter_context(tc.tile_pool(name="x", bufs=2 * CHUNKS))
        w_pool = ctx.enter_context(tc.tile_pool(name="w", bufs=2 * PASSES // W_LOAD))
        code_pool = ctx.enter_context(tc.tile_pool(name="codes", bufs=3))
        grouped_pool = ctx.enter_context(tc.tile_pool(name="grouped", bufs=3))
        work = ctx.enter_context(tc.tile_pool(name="work", bufs=2))
        score_pool = ctx.enter_context(tc.psum_pool(name="score", bufs=2))
        bank_pool = ctx.enter_context(tc.psum_pool(name="bank", bufs=6))
        ctx.enter_context(tc.manual_schedule())

        ident = keep.tile([P, P], F32)
        make_identity(nc, ident[:])
        w_planes = [zeroed_planes(nc, keep, t) for t in range(WINDOWS // TILE_WINDOWS)]

        lse = keep.tile([P, FEATURES], F32)
        avg = keep.tile([P, FEATURES], F32)

        bursts = scale_bursts()

        def load_x(w):
            return load_x_window(nc, x_pool, x, w, w_planes, template_flat_scales, bursts)

        def load_weights(w):
            return load_weight_window(nc, w_pool, template_flat_words, w, w_planes, template_flat_scales, bursts)

        def quantise(x_chunks):
            return quantise_x_window(nc, code_pool, grouped_pool, bank_pool, ident, x_chunks)

        def take_in(w, quantised, w_passes):
            score = score_pool.tile([P, FEATURES], F32, name="score")
            score_window(nc, score, quantised[0], quantised[1], w_passes, w_planes[w // TILE_WINDOWS], w)
            fold_window(nc, work, lse, avg, score, w)

        x_0 = load_x(0)
        quantised_0 = quantise(x_0)
        x_1 = load_x(1)
        weights_0 = load_weights(0)
        x_2 = load_x(2)
        quantised_1 = quantise(x_1)
        quantised_2 = quantise(x_2)
        take_in(0, quantised_0, weights_0)
        weights_1 = load_weights(1)
        take_in(1, quantised_1, weights_1)
        x_3 = load_x(3)
        quantised_3 = quantise(x_3)
        weights_2 = load_weights(2)
        take_in(2, quantised_2, weights_2)
        weights_3 = load_weights(3)
        take_in(3, quantised_3, weights_3)

        for cols in HALVES:
            nc.sync.dma_start(out=out[:, cols], in_=avg[:, cols])
